import numpy as np
import ml_dtypes


def mxq(x, axis, fmt="e4m3"):
    dtype, down = {"e4m3": (ml_dtypes.float8_e4m3fn, 7), "e5m2": (ml_dtypes.float8_e5m2, 14)}[fmt]
    v = np.moveaxis(np.asarray(x, np.float32).astype(ml_dtypes.bfloat16).astype(np.float64), axis, -1)
    blocks = v.reshape(v.shape[:-1] + (-1, 32))
    amax = np.abs(blocks).max(-1, keepdims=True)
    byte = np.maximum(np.where(amax > 0, np.frexp(amax)[1] - 1 + 127, 0) - down, 1)
    scale = np.exp2(byte - 127.0)
    codes = (blocks / scale).astype(np.float32).astype(dtype).astype(np.float64)
    return np.moveaxis((codes * scale).reshape(v.shape), -1, axis)


WIDE = False


def mx_kscale(k):
    if not WIDE:
        return np.ones(k)
    levels = np.array([10, -10, 5, -5, 0])
    a = np.random.permutation(np.resize(levels, k // 512 * 4)).reshape(k // 512, 4)
    idx = np.arange(k)
    return np.exp2(a[idx // 512, idx % 128 // 32])


BF16 = ml_dtypes.bfloat16


def bf(x):
    return np.asarray(x, np.float32).astype(BF16)


def f64(x):
    return np.asarray(x).astype(np.float64)


E2M1 = np.array([0.0, 0.5, 1.0, 1.5, 2.0, 3.0, 4.0, 6.0, -0.0, -0.5, -1.0, -1.5, -2.0, -3.0, -4.0, -6.0])


def pack_weight(w, fmt):
    k, n = w.shape
    w = f64(bf(w)).reshape(k // 32, 32, n)
    amax = np.abs(w).max(1)
    if fmt == "e4m3":
        byte = np.frexp(amax)[1] - 1 + 127 - 7
    else:
        mant, ex = np.frexp(amax / 6.0)
        byte = np.where(mant > 0.5, ex, ex - 1) + 127
    byte = np.clip(np.where(amax > 0, byte, 1), 1, 254)
    scaled = (w * np.exp2(127.0 - byte)[:, None, :]).reshape(k, n).astype(np.float32)
    by_word = np.ascontiguousarray(scaled.reshape(k // 512, 128, 4, n).transpose(0, 1, 3, 2))
    if fmt == "e4m3":
        words = by_word.astype(ml_dtypes.float8_e4m3fn).view(np.uint8)
    else:
        c = by_word.astype(ml_dtypes.float4_e2m1fn).view(np.uint8) & 0xF
        words = c[..., 0::2] | (c[..., 1::2] << 4)
    return np.ascontiguousarray(words), np.ascontiguousarray(byte.astype(np.uint8).reshape(k // 512, 16, n))


def unpack_weight(words, scales, fmt):
    g, p, n, _ = words.shape
    if fmt == "e4m3":
        vals = np.ascontiguousarray(words).view(ml_dtypes.float8_e4m3fn).astype(np.float64)
    else:
        nib = np.empty((g, p, n, 4), np.uint8)
        nib[..., 0::2] = words & 0xF
        nib[..., 1::2] = words >> 4
        vals = E2M1[nib]
    vals = vals * np.repeat(np.exp2(scales.astype(np.float64) - 127.0), 8, axis=1)[..., None]
    return vals.transpose(0, 1, 3, 2).reshape(g * 512, n)


E, C, H, I = 4, 2048, 512, 512
FMT = "e4m3"


def erf(z):
    z = np.clip(z, -6.0, 6.0)
    y = 2.0 * z * z
    acc = np.ones_like(z)
    for n in range(100, 0, -1):
        acc = 1.0 + acc * y / (2 * n + 1)
    return np.clip(2.0 / np.sqrt(np.pi) * z * np.exp(-z * z) * acc, -1.0, 1.0)


def gelu_erf(v):
    return 0.5 * v * (1.0 + erf(v / np.sqrt(2.0)))


def setup_inputs():
    s = mx_kscale(H)
    x = bf(np.random.standard_normal((E * C, H)) * s)
    w1 = np.random.standard_normal((E, H, I)) / np.sqrt(H) / s[:, None]
    w1_words, w1_scales = pack_weight(w1.reshape(-1, I), FMT)
    b1 = bf(np.random.standard_normal((E, I)) * 0.3)
    w2 = np.random.standard_normal((E, I, H)) * 1.5 / np.sqrt(I)
    w2_words, w2_scales = pack_weight(w2.reshape(-1, H), FMT)
    b2 = bf(np.random.standard_normal((E, H)) * 0.3)
    return {"x": x,
            "w1_words": w1_words,
            "w1_scales": w1_scales,
            "b1": b1,
            "w2_words": w2_words,
            "w2_scales": w2_scales,
            "b2": b2}


def reference(x, w1_words, w1_scales, b1, w2_words, w2_scales, b2):
    xe = f64(x).reshape(E, C, H)
    h = gelu_erf((mxq(xe, 2, "e4m3") @ unpack_weight(w1_words, w1_scales, FMT).reshape(E, H, I)) + f64(b1)[:, None, :])
    out = (mxq(h, 2, "e4m3") @ unpack_weight(w2_words, w2_scales, FMT).reshape(E, I, H)) + f64(b2)[:, None, :]
    return out.reshape(E * C, H)

@@ -1,0 +1,209 @@
+from contextlib import ExitStack
+
+import concourse.mybir as mybir
+from concourse.masks import make_identity
+
+F32 = mybir.dt.float32
+BF16 = mybir.dt.bfloat16
+I32 = mybir.dt.int32
+U32 = mybir.dt.uint32
+U8 = mybir.dt.uint8
+FP8X4 = mybir.dt.float8_e4m3fn_x4
+GELU = mybir.ActivationFunctionType.Gelu
+ADD = mybir.AluOpType.add
+
+P = 128
+PACK = 4
+EXPERTS = 4
+WIDTH = 512
+WORDS = WIDTH // 2
+TILES = 2
+UNITS = 32
+UNITS_PER_EXPERT = UNITS // EXPERTS
+UNITS_PER_LOAD = 2
+LOADS = UNITS // UNITS_PER_LOAD
+LOADS_PER_EXPERT = LOADS // EXPERTS
+PLANE_ROWS = 4
+
+FLOPS = 2 * 2 * UNITS * TILES * P * WIDTH * WIDTH
+
+
+def tile_fusedthorexpert_t_e_kernel(
+    tc, x, w1_words, w1_scales, b1, w2_words, w2_scales, b2, out
+):
+    nc = tc.nc
+    x_loads = x.rearrange("(l p j) k -> l p (j k)", p=P, j=UNITS_PER_LOAD * TILES)
+    out_units = out.rearrange("(l p v a) n -> l v p (a n)", p=P, v=UNITS_PER_LOAD, a=TILES)
+
+    with ExitStack() as ctx:
+        keep = ctx.enter_context(tc.tile_pool(name="keep", bufs=1))
+        work = ctx.enter_context(tc.tile_pool(name="work", bufs=2))
+        psum = ctx.enter_context(tc.psum_pool(name="psum", bufs=2))
+        ctx.enter_context(tc.manual_schedule())
+
+        ident = keep.tile([P, P], F32)
+        make_identity(nc, ident[:])
+
+        w1_planes = keep.tile([P, WIDTH], U8, align_bytes=64)
+        w2_planes = keep.tile([P, WIDTH], U8, align_bytes=64)
+        nc.vector.memset(w1_planes[:].bitcast(I32), 0)
+        nc.vector.memset(w2_planes[:].bitcast(I32), 0)
+        w1_codes = keep.tile([P, EXPERTS, PACK * WIDTH], U8, align_bytes=64)
+        w2_codes = keep.tile([P, EXPERTS, PACK * WIDTH], U8, align_bytes=64)
+        b1_rows = keep.tile([P, EXPERTS, WIDTH], BF16)
+        b2_rows = keep.tile([P, EXPERTS, WIDTH], BF16)
+        x_tiles = [
+            keep.tile([P, UNITS_PER_LOAD * TILES, WIDTH], BF16, name="x%d" % l) for l in range(LOADS)
+        ]
+
+        def load_x(l):
+            nc.sync.dma_start(out=x_tiles[l][:].rearrange("p j k -> p (j k)"), in_=x_loads[l])
+
+        def load_codes(codes, words, e):
+            nc.sync.dma_start(
+                out=codes[:, e, :].bitcast(I32),
+                in_=words[e].rearrange("p n t -> p (n t)").bitcast(I32),
+            )
+
+        def load_planes(planes, scales):
+            for quadrant in range(4):
+                rows = slice(PLANE_ROWS * quadrant, PLANE_ROWS * (quadrant + 1))
+                first = 32 * quadrant
+                nc.sync.dma_start(
+                    out=planes[first : first + EXPERTS * PLANE_ROWS, :].bitcast(I32),
+                    in_=scales[:, rows, :].bitcast(I32),
+                )
+
+        for rows, bias in ((b1_rows, b1), (b2_rows, b2)):
+            nc.scalar.dma_start(
+                out=rows[:].rearrange("p e i -> p (e i)"),
+                in_=bias.rearrange("e i -> (e i)").partition_broadcast(P),
+            )
+
+        warm = keep.tile([P, 1], F32)
+        nc.vector.memset(warm[:], 0.0)
+        nc.scalar.activation(out=warm[:], in_=warm[:], func=GELU)
+
+        load_x(0)
+        load_codes(w1_codes, w1_words, 0)
+        load_planes(w1_planes, w1_scales)
+        load_x(1)
+        load_codes(w2_codes, w2_words, 0)
+        load_planes(w2_planes, w2_scales)
+        load_x(2)
+        load_x(3)
+        for e in range(1, EXPERTS):
+            load_codes(w1_codes, w1_words, e)
+            load_codes(w2_codes, w2_words, e)
+            for l in range(LOADS_PER_EXPERT * e, LOADS_PER_EXPERT * (e + 1)):
+                load_x(l)
+
+        def transpose_words(rows_of_tile, tag):
+            bank = psum.tile([P, TILES, 2, P], F32, tag=tag, name=tag)
+            for a in range(TILES):
+                words = rows_of_tile(a).bitcast(F32)
+                for half in range(2):
+                    nc.tensor.transpose(
+                        out=bank[:, a, half, :], in_=words[:, half:WORDS:2], identity=ident[:]
+                    )
+            return bank
+
+        def regroup(bank, tag):
+            grouped = work.tile([P, TILES * P * PACK], BF16, tag=tag, name=tag, align_bytes=64)
+            nc.scalar.copy(
+                out=grouped[:].bitcast(F32).rearrange("p (a t w) -> p a t w", a=TILES, w=2),
+                in_=bank[:].rearrange("p a w t -> p a t w"),
+            )
+            return grouped
+
+        def quantise(grouped, tag):
+            codes = work.tile(
+                [P, TILES * P], U32, tag=tag + "_codes", name=tag + "_codes", bufs=3, align_bytes=64
+            )
+            plane = work.tile(
+                [P, TILES * P], U8, tag=tag + "_plane", name=tag + "_plane", bufs=3, align_bytes=64
+            )
+            nc.vector.quantize_mx(out=codes[:].bitcast(FP8X4), scales=plane[:], in_=grouped[:])
+            return codes, plane
+
+        def multiply(tokens, a, w_codes, w_planes, e, tag):
+            codes, plane = tokens
+            cols = slice(P * a, P * (a + 1))
+            acc = psum.tile([P, WIDTH], F32, tag=tag, name=tag)
+            nc.tensor.matmul_mx(
+                out=acc[:],
+                lhsT=codes[:, cols].bitcast(FP8X4),
+                lhsT_scale=plane[:, cols],
+                rhs=w_codes[:, e, :].bitcast(FP8X4),
+                rhs_scale=w_planes[PLANE_ROWS * e : P, :],
+                start=True,
+                stop=True,
+            )
+            return acc
+
+        x_grouped, x_mx, first_sums = {}, {}, {}
+        h_tiles, h_grouped, h_mx, second_sums = {}, {}, {}, {}
+
+        def is_unit(u):
+            return 0 <= u < UNITS
+
+        def x_onto_partitions(u):
+            rows = x_tiles[u // UNITS_PER_LOAD]
+            first = TILES * (u % UNITS_PER_LOAD)
+            x_grouped[u] = regroup(transpose_words(lambda a: rows[:, first + a, :], "xt"), "x_grouped")
+
+        def h_onto_partitions(u):
+            h_grouped[u] = regroup(transpose_words(lambda a: h_tiles[(u, a)][:], "ht"), "h_grouped")
+
+        def first_product(u, a):
+            first_sums[(u, a)] = multiply(x_mx[u], a, w1_codes, w1_planes, u // UNITS_PER_EXPERT, "z")
+
+        def first_finish(u, a):
+            biased = work.tile([P, WIDTH], F32, tag="biased", name="biased", bufs=3)
+            nc.vector.tensor_tensor(
+                out=biased[:],
+                in0=first_sums[(u, a)][:],
+                in1=b1_rows[:, u // UNITS_PER_EXPERT, :],
+                op=ADD,
+            )
+            h = work.tile([P, WIDTH], BF16, tag="h", name="h", bufs=3 * TILES)
+            nc.scalar.activation(out=h[:], in_=biased[:], func=GELU)
+            h_tiles[(u, a)] = h
+
+        def second_product(u, a):
+            second_sums[(u, a)] = multiply(h_mx[u], a, w2_codes, w2_planes, u // UNITS_PER_EXPERT, "o")
+
+        def second_finish(u, a, result):
+            nc.vector.tensor_tensor(
+                out=result[:, a, :],
+                in0=second_sums[(u, a)][:],
+                in1=b2_rows[:, u // UNITS_PER_EXPERT, :],
+                op=ADD,
+            )
+
+        for s in range(-3, UNITS + 2):
+            for a in range(TILES):
+                if is_unit(s):
+                    first_finish(s, a)
+                if is_unit(s + 1):
+                    first_product(s + 1, a)
+            if is_unit(s + 3):
+                x_onto_partitions(s + 3)
+            if is_unit(s):
+                h_onto_partitions(s)
+            if is_unit(s - 1):
+                h_mx[s - 1] = quantise(h_grouped[s - 1], "h")
+            if is_unit(s + 2):
+                x_mx[s + 2] = quantise(x_grouped[s + 2], "x")
+            if is_unit(s - 2):
+                result = work.tile([P, TILES, WIDTH], F32, tag="result", name="result", bufs=4)
+            for a in range(TILES):
+                if is_unit(s - 2):
+                    second_finish(s - 2, a, result)
+                if is_unit(s - 1):
+                    second_product(s - 1, a)
+            if is_unit(s - 2):
+                nc.sync.dma_start(
+                    out=out_units[(s - 2) // UNITS_PER_LOAD, (s - 2) % UNITS_PER_LOAD],
+                    in_=result[:].rearrange("p a n -> p (a n)"),
+                )

@@ -109,7 +109,7 @@ def tile_fusedthorexpert_t_e_kernel(
             return bank
 
         def regroup(bank, tag):
-            grouped = work.tile([P, TILES * P * PACK], BF16, tag=tag, name=tag, align_bytes=64)
+            grouped = work.tile([P, TILES * P * PACK], BF16, tag=tag, name=tag, bufs=3, align_bytes=64)
             nc.scalar.copy(
                 out=grouped[:].bitcast(F32).rearrange("p (a t w) -> p a t w", a=TILES, w=2),
                 in_=bank[:].rearrange("p a w t -> p a t w"),
@@ -141,69 +141,82 @@ def tile_fusedthorexpert_t_e_kernel(
             )
             return acc
 
-        x_grouped, x_mx, first_sums = {}, {}, {}
-        h_tiles, h_grouped, h_mx, second_sums = {}, {}, {}, {}
+        x_banks, x_grouped, x_mx, first_sums, biased_tiles = {}, {}, {}, {}, {}
+        h_tiles, h_banks, h_grouped, h_mx, second_sums, results = {}, {}, {}, {}, {}, {}
 
         def is_unit(u):
             return 0 <= u < UNITS
 
-        def x_onto_partitions(u):
+        def x_rows(u):
             rows = x_tiles[u // UNITS_PER_LOAD]
             first = TILES * (u % UNITS_PER_LOAD)
-            x_grouped[u] = regroup(transpose_words(lambda a: rows[:, first + a, :], "xt"), "x_grouped")
+            return lambda a: rows[:, first + a, :]
 
-        def h_onto_partitions(u):
-            h_grouped[u] = regroup(transpose_words(lambda a: h_tiles[(u, a)][:], "ht"), "h_grouped")
+        def h_rows(u):
+            return lambda a: h_tiles[u][:, a, :]
 
         def first_product(u, a):
             first_sums[(u, a)] = multiply(x_mx[u], a, w1_codes, w1_planes, u // UNITS_PER_EXPERT, "z")
 
-        def first_finish(u, a):
-            biased = work.tile([P, WIDTH], F32, tag="biased", name="biased", bufs=3)
+        def add_b1(u, a):
+            if a == 0:
+                biased_tiles[u] = work.tile(
+                    [P, TILES, WIDTH], F32, tag="biased", name="biased", bufs=3
+                )
             nc.vector.tensor_tensor(
-                out=biased[:],
+                out=biased_tiles[u][:, a, :],
                 in0=first_sums[(u, a)][:],
                 in1=b1_rows[:, u // UNITS_PER_EXPERT, :],
                 op=ADD,
             )
-            h = work.tile([P, WIDTH], BF16, tag="h", name="h", bufs=3 * TILES)
-            nc.scalar.activation(out=h[:], in_=biased[:], func=GELU)
-            h_tiles[(u, a)] = h
+
+        def gelu(u):
+            h_tiles[u] = work.tile([P, TILES, WIDTH], BF16, tag="h", name="h", bufs=3)
+            nc.scalar.activation(out=h_tiles[u][:], in_=biased_tiles[u][:], func=GELU)
 
         def second_product(u, a):
             second_sums[(u, a)] = multiply(h_mx[u], a, w2_codes, w2_planes, u // UNITS_PER_EXPERT, "o")
 
-        def second_finish(u, a, result):
+        def add_b2(u, a):
+            if a == 0:
+                results[u] = work.tile([P, TILES, WIDTH], F32, tag="result", name="result", bufs=4)
             nc.vector.tensor_tensor(
-                out=result[:, a, :],
+                out=results[u][:, a, :],
                 in0=second_sums[(u, a)][:],
                 in1=b2_rows[:, u // UNITS_PER_EXPERT, :],
                 op=ADD,
             )
 
-        for s in range(-3, UNITS + 2):
+        def store(u):
+            nc.sync.dma_start(
+                out=out_units[u // UNITS_PER_LOAD, u % UNITS_PER_LOAD],
+                in_=results[u][:].rearrange("p a n -> p (a n)"),
+            )
+
+        for s in range(-4, UNITS + 7):
+            if is_unit(s - 1):
+                gelu(s - 1)
+            if is_unit(s + 3):
+                x_grouped[s + 3] = regroup(x_banks[s + 3], "x_grouped")
+            if is_unit(s - 3):
+                h_grouped[s - 3] = regroup(h_banks[s - 3], "h_grouped")
             for a in range(TILES):
                 if is_unit(s):
-                    first_finish(s, a)
+                    add_b1(s, a)
                 if is_unit(s + 1):
                     first_product(s + 1, a)
-            if is_unit(s + 3):
-                x_onto_partitions(s + 3)
-            if is_unit(s):
-                h_onto_partitions(s)
-            if is_unit(s - 1):
-                h_mx[s - 1] = quantise(h_grouped[s - 1], "h")
+            if is_unit(s + 4):
+                x_banks[s + 4] = transpose_words(x_rows(s + 4), "xt")
+            if is_unit(s - 2):
+                h_banks[s - 2] = transpose_words(h_rows(s - 2), "ht")
+            if is_unit(s - 4):
+                h_mx[s - 4] = quantise(h_grouped[s - 4], "h")
             if is_unit(s + 2):
                 x_mx[s + 2] = quantise(x_grouped[s + 2], "x")
-            if is_unit(s - 2):
-                result = work.tile([P, TILES, WIDTH], F32, tag="result", name="result", bufs=4)
             for a in range(TILES):
-                if is_unit(s - 2):
-                    second_finish(s - 2, a, result)
-                if is_unit(s - 1):
-                    second_product(s - 1, a)
-            if is_unit(s - 2):
-                nc.sync.dma_start(
-                    out=out_units[(s - 2) // UNITS_PER_LOAD, (s - 2) % UNITS_PER_LOAD],
-                    in_=result[:].rearrange("p a n -> p (a n)"),
-                )
+                if is_unit(s - 6):
+                    add_b2(s - 6, a)
+                if is_unit(s - 5):
+                    second_product(s - 5, a)
+            if is_unit(s - 6):
+                store(s - 6)

@@ -177,9 +177,19 @@ def tile_fusedthorexpert_t_e_kernel(
         def second_product(u, a):
             second_sums[(u, a)] = multiply(h_mx[u], a, w2_codes, w2_planes, u // UNITS_PER_EXPERT, "o")
 
+        def shared_out(u, a):
+            return u % 2 == 1 and a == 1
+
+        def add_b2_beside_vector(u, a):
+            nc.scalar.copy(out=results[u][:, a, :], in_=second_sums[(u, a)][:])
+            nc.gpsimd.tensor_tensor(
+                out=results[u][:, a, :],
+                in0=results[u][:, a, :],
+                in1=b2_rows[:, u // UNITS_PER_EXPERT, :],
+                op=ADD,
+            )
+
         def add_b2(u, a):
-            if a == 0:
-                results[u] = work.tile([P, TILES, WIDTH], F32, tag="result", name="result", bufs=4)
             nc.vector.tensor_tensor(
                 out=results[u][:, a, :],
                 in0=second_sums[(u, a)][:],
@@ -196,6 +206,13 @@ def tile_fusedthorexpert_t_e_kernel(
         for s in range(-4, UNITS + 7):
             if is_unit(s - 1):
                 gelu(s - 1)
+            if is_unit(s - 6):
+                results[s - 6] = work.tile(
+                    [P, TILES, WIDTH], F32, tag="result", name="result", bufs=4
+                )
+                for a in range(TILES):
+                    if shared_out(s - 6, a):
+                        add_b2_beside_vector(s - 6, a)
             if is_unit(s + 3):
                 x_grouped[s + 3] = regroup(x_banks[s + 3], "x_grouped")
             if is_unit(s - 3):
@@ -214,7 +231,7 @@ def tile_fusedthorexpert_t_e_kernel(
             if is_unit(s + 2):
                 x_mx[s + 2] = quantise(x_grouped[s + 2], "x")
             for a in range(TILES):
-                if is_unit(s - 6):
+                if is_unit(s - 6) and not shared_out(s - 6, a):
                     add_b2(s - 6, a)
                 if is_unit(s - 5):
                     second_product(s - 5, a)

@@ -98,13 +98,12 @@ def tile_fusedthorexpert_t_e_kernel(
             for l in range(LOADS_PER_EXPERT * e, LOADS_PER_EXPERT * (e + 1)):
                 load_x(l)
 
-        def transpose_words(rows_of_tile, tag):
+        def transpose_words(words_of_tile, tag):
             bank = psum.tile([P, TILES, 2, P], F32, tag=tag, name=tag)
             for a in range(TILES):
-                words = rows_of_tile(a).bitcast(F32)
-                for half in range(2):
+                for w in range(2):
                     nc.tensor.transpose(
-                        out=bank[:, a, half, :], in_=words[:, half:WORDS:2], identity=ident[:]
+                        out=bank[:, a, w, :], in_=words_of_tile(a, w), identity=ident[:]
                     )
             return bank
 
@@ -147,13 +146,16 @@ def tile_fusedthorexpert_t_e_kernel(
         def is_unit(u):
             return 0 <= u < UNITS
 
-        def x_rows(u):
+        def x_words(u):
             rows = x_tiles[u // UNITS_PER_LOAD]
             first = TILES * (u % UNITS_PER_LOAD)
-            return lambda a: rows[:, first + a, :]
+            return lambda a, w: rows[:, first + a, :].bitcast(F32)[:, w:WORDS:2]
 
-        def h_rows(u):
-            return lambda a: h_tiles[u][:, a, :]
+        def h_words(u):
+            return lambda a, w: h_tiles[u][:, a, :].bitcast(F32)[:, P * w : P * (w + 1)]
+
+        def even_words_first(row):
+            return row.rearrange("p (q w c) -> p w q c", w=2, c=2)
 
         def first_product(u, a):
             first_sums[(u, a)] = multiply(x_mx[u], a, w1_codes, w1_planes, u // UNITS_PER_EXPERT, "z")
@@ -164,9 +166,9 @@ def tile_fusedthorexpert_t_e_kernel(
                     [P, TILES, WIDTH], F32, tag="biased", name="biased", bufs=3
                 )
             nc.vector.tensor_tensor(
-                out=biased_tiles[u][:, a, :],
-                in0=first_sums[(u, a)][:],
-                in1=b1_rows[:, u // UNITS_PER_EXPERT, :],
+                out=biased_tiles[u][:, a, :].rearrange("p (w q c) -> p w q c", w=2, c=2),
+                in0=even_words_first(first_sums[(u, a)][:]),
+                in1=even_words_first(b1_rows[:, u // UNITS_PER_EXPERT, :]),
                 op=ADD,
             )
 
@@ -223,9 +225,9 @@ def tile_fusedthorexpert_t_e_kernel(
                 if is_unit(s + 1):
                     first_product(s + 1, a)
             if is_unit(s + 4):
-                x_banks[s + 4] = transpose_words(x_rows(s + 4), "xt")
+                x_banks[s + 4] = transpose_words(x_words(s + 4), "xt")
             if is_unit(s - 2):
-                h_banks[s - 2] = transpose_words(h_rows(s - 2), "ht")
+                h_banks[s - 2] = transpose_words(h_words(s - 2), "ht")
             if is_unit(s - 4):
                 h_mx[s - 4] = quantise(h_grouped[s - 4], "h")
             if is_unit(s + 2):

@@ -20,9 +20,6 @@ WORDS = WIDTH // 2
 TILES = 2
 UNITS = 32
 UNITS_PER_EXPERT = UNITS // EXPERTS
-UNITS_PER_LOAD = 2
-LOADS = UNITS // UNITS_PER_LOAD
-LOADS_PER_EXPERT = LOADS // EXPERTS
 PLANE_ROWS = 4
 
 FLOPS = 2 * 2 * UNITS * TILES * P * WIDTH * WIDTH
@@ -32,8 +29,8 @@ def tile_fusedthorexpert_t_e_kernel(
     tc, x, w1_words, w1_scales, b1, w2_words, w2_scales, b2, out
 ):
     nc = tc.nc
-    x_loads = x.rearrange("(l p j) k -> l p (j k)", p=P, j=UNITS_PER_LOAD * TILES)
-    out_units = out.rearrange("(l p v a) n -> l v p (a n)", p=P, v=UNITS_PER_LOAD, a=TILES)
+    x_units = x.rearrange("(u p a) k -> u p (a k)", p=P, a=TILES)
+    out_units = out.rearrange("(u p a) n -> u p (a n)", p=P, a=TILES)
 
     with ExitStack() as ctx:
         keep = ctx.enter_context(tc.tile_pool(name="keep", bufs=1))
@@ -52,12 +49,10 @@ def tile_fusedthorexpert_t_e_kernel(
         w2_codes = keep.tile([P, EXPERTS, PACK * WIDTH], U8, align_bytes=64)
         b1_rows = keep.tile([P, EXPERTS, WIDTH], BF16)
         b2_rows = keep.tile([P, EXPERTS, WIDTH], BF16)
-        x_tiles = [
-            keep.tile([P, UNITS_PER_LOAD * TILES, WIDTH], BF16, name="x%d" % l) for l in range(LOADS)
-        ]
+        x_tiles = [keep.tile([P, TILES, WIDTH], BF16, name="x%d" % u) for u in range(UNITS)]
 
-        def load_x(l):
-            nc.sync.dma_start(out=x_tiles[l][:].rearrange("p j k -> p (j k)"), in_=x_loads[l])
+        def load_x(u):
+            nc.sync.dma_start(out=x_tiles[u][:].rearrange("p a k -> p (a k)"), in_=x_units[u])
 
         def load_codes(codes, words, e):
             nc.sync.dma_start(
@@ -90,13 +85,13 @@ def tile_fusedthorexpert_t_e_kernel(
         load_x(1)
         load_codes(w2_codes, w2_words, 0)
         load_planes(w2_planes, w2_scales)
-        load_x(2)
-        load_x(3)
+        for u in range(2, UNITS_PER_EXPERT):
+            load_x(u)
         for e in range(1, EXPERTS):
             load_codes(w1_codes, w1_words, e)
             load_codes(w2_codes, w2_words, e)
-            for l in range(LOADS_PER_EXPERT * e, LOADS_PER_EXPERT * (e + 1)):
-                load_x(l)
+            for u in range(UNITS_PER_EXPERT * e, UNITS_PER_EXPERT * (e + 1)):
+                load_x(u)
 
         def transpose_words(words_of_tile, tag):
             bank = psum.tile([P, TILES, 2, P], F32, tag=tag, name=tag)
@@ -125,10 +120,10 @@ def tile_fusedthorexpert_t_e_kernel(
             nc.vector.quantize_mx(out=codes[:].bitcast(FP8X4), scales=plane[:], in_=grouped[:])
             return codes, plane
 
-        def multiply(tokens, a, w_codes, w_planes, e, tag):
+        def multiply(tokens, a, w_codes, w_planes, e):
             codes, plane = tokens
             cols = slice(P * a, P * (a + 1))
-            acc = psum.tile([P, WIDTH], F32, tag=tag, name=tag)
+            acc = psum.tile([P, WIDTH], F32, tag="sums", name="sums", bufs=4)
             nc.tensor.matmul_mx(
                 out=acc[:],
                 lhsT=codes[:, cols].bitcast(FP8X4),
@@ -147,9 +142,7 @@ def tile_fusedthorexpert_t_e_kernel(
             return 0 <= u < UNITS
 
         def x_words(u):
-            rows = x_tiles[u // UNITS_PER_LOAD]
-            first = TILES * (u % UNITS_PER_LOAD)
-            return lambda a, w: rows[:, first + a, :].bitcast(F32)[:, w:WORDS:2]
+            return lambda a, w: x_tiles[u][:, a, :].bitcast(F32)[:, w:WORDS:2]
 
         def h_words(u):
             return lambda a, w: h_tiles[u][:, a, :].bitcast(F32)[:, P * w : P * (w + 1)]
@@ -158,7 +151,7 @@ def tile_fusedthorexpert_t_e_kernel(
             return row.rearrange("p (q w c) -> p w q c", w=2, c=2)
 
         def first_product(u, a):
-            first_sums[(u, a)] = multiply(x_mx[u], a, w1_codes, w1_planes, u // UNITS_PER_EXPERT, "z")
+            first_sums[(u, a)] = multiply(x_mx[u], a, w1_codes, w1_planes, u // UNITS_PER_EXPERT)
 
         def add_b1(u, a):
             if a == 0:
@@ -177,10 +170,10 @@ def tile_fusedthorexpert_t_e_kernel(
             nc.scalar.activation(out=h_tiles[u][:], in_=biased_tiles[u][:], func=GELU)
 
         def second_product(u, a):
-            second_sums[(u, a)] = multiply(h_mx[u], a, w2_codes, w2_planes, u // UNITS_PER_EXPERT, "o")
+            second_sums[(u, a)] = multiply(h_mx[u], a, w2_codes, w2_planes, u // UNITS_PER_EXPERT)
 
         def shared_out(u, a):
-            return u % 2 == 1 and a == 1
+            return u % 2 == 0 and a == 0
 
         def add_b2_beside_vector(u, a):
             nc.scalar.copy(out=results[u][:, a, :], in_=second_sums[(u, a)][:])
@@ -201,7 +194,7 @@ def tile_fusedthorexpert_t_e_kernel(
 
         def store(u):
             nc.sync.dma_start(
-                out=out_units[u // UNITS_PER_LOAD, u % UNITS_PER_LOAD],
+                out=out_units[u],
                 in_=results[u][:].rearrange("p a n -> p (a n)"),
             )
 

@@ -17,20 +17,25 @@ PACK = 4
 EXPERTS = 4
 WIDTH = 512
 WORDS = WIDTH // 2
-TILES = 2
-UNITS = 32
-UNITS_PER_EXPERT = UNITS // EXPERTS
+TOKENS = 8192
 PLANE_ROWS = 4
 
-FLOPS = 2 * 2 * UNITS * TILES * P * WIDTH * WIDTH
+UNIT_TILES = [2, 2, 4, 4, 4] + [4] * 8 + [4, 4, 4, 2, 2]
+UNITS = len(UNIT_TILES)
+FIRST_TILE = [sum(UNIT_TILES[:u]) for u in range(UNITS)]
+EXPERT_OF = [FIRST_TILE[u] // 16 for u in range(UNITS)]
+
+FLOPS = 2 * 2 * TOKENS * WIDTH * WIDTH
 
 
 def tile_fusedthorexpert_t_e_kernel(
     tc, x, w1_words, w1_scales, b1, w2_words, w2_scales, b2, out
 ):
     nc = tc.nc
-    x_units = x.rearrange("(u p a) k -> u p (a k)", p=P, a=TILES)
-    out_units = out.rearrange("(u p a) n -> u p (a n)", p=P, a=TILES)
+
+    def rows_of(array, u):
+        rows = slice(P * FIRST_TILE[u], P * (FIRST_TILE[u] + UNIT_TILES[u]))
+        return array[rows, :].rearrange("(p a) k -> p (a k)", p=P)
 
     with ExitStack() as ctx:
         keep = ctx.enter_context(tc.tile_pool(name="keep", bufs=1))
@@ -41,23 +46,26 @@ def tile_fusedthorexpert_t_e_kernel(
         ident = keep.tile([P, P], F32)
         make_identity(nc, ident[:])
 
+        w1_planes_raw = keep.tile([P, WIDTH], U8, align_bytes=64)
         w1_planes = keep.tile([P, WIDTH], U8, align_bytes=64)
         w2_planes = keep.tile([P, WIDTH], U8, align_bytes=64)
-        nc.vector.memset(w1_planes[:].bitcast(I32), 0)
+        nc.vector.memset(w1_planes_raw[:].bitcast(I32), 0)
         nc.vector.memset(w2_planes[:].bitcast(I32), 0)
-        w1_codes = keep.tile([P, EXPERTS, PACK * WIDTH], U8, align_bytes=64)
-        w2_codes = keep.tile([P, EXPERTS, PACK * WIDTH], U8, align_bytes=64)
-        b1_rows = keep.tile([P, EXPERTS, WIDTH], BF16)
+        w1_raw = keep.tile([P, EXPERTS, WIDTH], I32, align_bytes=64)
+        w1_codes = keep.tile([P, EXPERTS, WIDTH], I32, align_bytes=64)
+        w2_codes = keep.tile([P, EXPERTS, WIDTH], I32, align_bytes=64)
+        b1_cols = keep.tile([P, EXPERTS, PACK], BF16)
         b2_rows = keep.tile([P, EXPERTS, WIDTH], BF16)
-        x_tiles = [keep.tile([P, TILES, WIDTH], BF16, name="x%d" % u) for u in range(UNITS)]
+        x_tiles = [
+            keep.tile([P, UNIT_TILES[u], WIDTH], BF16, name="x%d" % u) for u in range(UNITS)
+        ]
 
         def load_x(u):
-            nc.sync.dma_start(out=x_tiles[u][:].rearrange("p a k -> p (a k)"), in_=x_units[u])
+            nc.sync.dma_start(out=x_tiles[u][:].rearrange("p a k -> p (a k)"), in_=rows_of(x, u))
 
         def load_codes(codes, words, e):
             nc.sync.dma_start(
-                out=codes[:, e, :].bitcast(I32),
-                in_=words[e].rearrange("p n t -> p (n t)").bitcast(I32),
+                out=codes[:, e, :], in_=words[e].rearrange("p n t -> p (n t)").bitcast(I32)
             )
 
         def load_planes(planes, scales):
@@ -69,166 +77,174 @@ def tile_fusedthorexpert_t_e_kernel(
                     in_=scales[:, rows, :].bitcast(I32),
                 )
 
-        for rows, bias in ((b1_rows, b1), (b2_rows, b2)):
-            nc.scalar.dma_start(
-                out=rows[:].rearrange("p e i -> p (e i)"),
-                in_=bias.rearrange("e i -> (e i)").partition_broadcast(P),
-            )
-
         warm = keep.tile([P, 1], F32)
         nc.vector.memset(warm[:], 0.0)
         nc.scalar.activation(out=warm[:], in_=warm[:], func=GELU)
 
         load_x(0)
-        load_codes(w1_codes, w1_words, 0)
-        load_planes(w1_planes, w1_scales)
+        load_codes(w1_raw, w1_words, 0)
+        load_planes(w1_planes_raw, w1_scales)
+        nc.scalar.dma_start(out=b1_cols[:], in_=b1.rearrange("e (p t) -> p e t", t=PACK))
         load_x(1)
         load_codes(w2_codes, w2_words, 0)
         load_planes(w2_planes, w2_scales)
-        for u in range(2, UNITS_PER_EXPERT):
+        load_x(2)
+        nc.sync.dma_start(
+            out=b2_rows[:].rearrange("p e i -> p (e i)"),
+            in_=b2.rearrange("e i -> (e i)").partition_broadcast(P),
+        )
+        for u in range(3, UNITS):
+            if EXPERT_OF[u] != EXPERT_OF[u - 1]:
+                load_codes(w1_raw, w1_words, EXPERT_OF[u])
+                load_codes(w2_codes, w2_words, EXPERT_OF[u])
             load_x(u)
-        for e in range(1, EXPERTS):
-            load_codes(w1_codes, w1_words, e)
-            load_codes(w2_codes, w2_words, e)
-            for u in range(UNITS_PER_EXPERT * e, UNITS_PER_EXPERT * (e + 1)):
-                load_x(u)
 
-        def transpose_words(words_of_tile, tag):
-            bank = psum.tile([P, TILES, 2, P], F32, tag=tag, name=tag)
-            for a in range(TILES):
-                for w in range(2):
-                    nc.tensor.transpose(
-                        out=bank[:, a, w, :], in_=words_of_tile(a, w), identity=ident[:]
-                    )
-            return bank
-
-        def regroup(bank, tag):
-            grouped = work.tile([P, TILES * P * PACK], BF16, tag=tag, name=tag, bufs=3, align_bytes=64)
-            nc.scalar.copy(
-                out=grouped[:].bitcast(F32).rearrange("p (a t w) -> p a t w", a=TILES, w=2),
-                in_=bank[:].rearrange("p a w t -> p a t w"),
+        def sort_codes(e):
+            nc.vector.tensor_copy(
+                out=w1_codes[:, e, :].rearrange("p (t m) -> p t m", t=PACK),
+                in_=w1_raw[:, e, :].rearrange("p (m t) -> p t m", t=PACK),
             )
-            return grouped
 
-        def quantise(grouped, tag):
-            codes = work.tile(
-                [P, TILES * P], U32, tag=tag + "_codes", name=tag + "_codes", bufs=3, align_bytes=64
-            )
-            plane = work.tile(
-                [P, TILES * P], U8, tag=tag + "_plane", name=tag + "_plane", bufs=3, align_bytes=64
-            )
-            nc.vector.quantize_mx(out=codes[:].bitcast(FP8X4), scales=plane[:], in_=grouped[:])
-            return codes, plane
+        nc.vector.tensor_copy(
+            out=w1_planes[:].rearrange("p (t m) -> p t m", t=PACK),
+            in_=w1_planes_raw[:].rearrange("p (m t) -> p t m", t=PACK),
+        )
+        sort_codes(0)
 
-        def multiply(tokens, a, w_codes, w_planes, e):
-            codes, plane = tokens
-            cols = slice(P * a, P * (a + 1))
-            acc = psum.tile([P, WIDTH], F32, tag="sums", name="sums", bufs=4)
-            nc.tensor.matmul_mx(
-                out=acc[:],
-                lhsT=codes[:, cols].bitcast(FP8X4),
-                lhsT_scale=plane[:, cols],
-                rhs=w_codes[:, e, :].bitcast(FP8X4),
-                rhs_scale=w_planes[PLANE_ROWS * e : P, :],
-                start=True,
-                stop=True,
-            )
-            return acc
-
-        x_banks, x_grouped, x_mx, first_sums, biased_tiles = {}, {}, {}, {}, {}
-        h_tiles, h_banks, h_grouped, h_mx, second_sums, results = {}, {}, {}, {}, {}, {}
+        x_banks, x_grouped, x_mx, first_sums = {}, {}, {}, {}
+        h_tiles, h_grouped, h_mx, second_sums, results = {}, {}, {}, {}, {}
 
         def is_unit(u):
             return 0 <= u < UNITS
 
-        def x_words(u):
-            return lambda a, w: x_tiles[u][:, a, :].bitcast(F32)[:, w:WORDS:2]
+        def transpose_x(u):
+            for a in range(UNIT_TILES[u]):
+                if a % 2 == 0:
+                    bank = psum.tile([P, 2, 2, P], F32, tag="xt", name="xt", bufs=2)
+                    x_banks[(u, a // 2)] = bank
+                words = x_tiles[u][:, a, :].bitcast(F32)
+                for w in range(2):
+                    nc.tensor.transpose(
+                        out=bank[:, a % 2, w, :], in_=words[:, w:WORDS:2], identity=ident[:]
+                    )
 
-        def h_words(u):
-            return lambda a, w: h_tiles[u][:, a, :].bitcast(F32)[:, P * w : P * (w + 1)]
-
-        def even_words_first(row):
-            return row.rearrange("p (q w c) -> p w q c", w=2, c=2)
-
-        def first_product(u, a):
-            first_sums[(u, a)] = multiply(x_mx[u], a, w1_codes, w1_planes, u // UNITS_PER_EXPERT)
-
-        def add_b1(u, a):
-            if a == 0:
-                biased_tiles[u] = work.tile(
-                    [P, TILES, WIDTH], F32, tag="biased", name="biased", bufs=3
+        def regroup_x(u, half):
+            if half == 0:
+                x_grouped[u] = work.tile(
+                    [P, UNIT_TILES[u] * P * PACK], BF16, tag="xg", name="xg", align_bytes=64
                 )
-            nc.vector.tensor_tensor(
-                out=biased_tiles[u][:, a, :].rearrange("p (w q c) -> p w q c", w=2, c=2),
-                in0=even_words_first(first_sums[(u, a)][:]),
-                in1=even_words_first(b1_rows[:, u // UNITS_PER_EXPERT, :]),
-                op=ADD,
+            size = 2 * P * PACK
+            part = x_grouped[u][:, size * half : size * (half + 1)]
+            nc.scalar.copy(
+                out=part.bitcast(F32).rearrange("p (a t w) -> p a t w", a=2, w=2),
+                in_=x_banks[(u, half)][:].rearrange("p a w t -> p a t w"),
             )
 
-        def gelu(u):
-            h_tiles[u] = work.tile([P, TILES, WIDTH], BF16, tag="h", name="h", bufs=3)
-            nc.scalar.activation(out=h_tiles[u][:], in_=biased_tiles[u][:], func=GELU)
+        def quantise(grouped, u, tag):
+            codes = work.tile(
+                [P, UNIT_TILES[u] * P], U32, tag=tag + "_codes", name=tag + "_codes", align_bytes=64
+            )
+            plane = work.tile(
+                [P, UNIT_TILES[u] * P], U8, tag=tag + "_plane", name=tag + "_plane", align_bytes=64
+            )
+            nc.vector.quantize_mx(out=codes[:].bitcast(FP8X4), scales=plane[:], in_=grouped[:])
+            return codes, plane
+
+        def first_product(u, t):
+            e = EXPERT_OF[u]
+            codes, plane = x_mx[u]
+            cols = slice(P * t, P * (t + 1))
+            acc = psum.tile([P, UNIT_TILES[u] * P], F32, tag="first", name="first", bufs=3)
+            nc.tensor.matmul_mx(
+                out=acc[:],
+                lhsT=w1_codes[:, e, cols].bitcast(FP8X4),
+                lhsT_scale=w1_planes[PLANE_ROWS * e : P, cols],
+                rhs=codes[:].bitcast(FP8X4),
+                rhs_scale=plane[:],
+                start=True,
+                stop=True,
+            )
+            first_sums[(u, t)] = acc
+
+        def gelu(u, t):
+            if t == 0:
+                h_tiles[u] = work.tile([P, PACK, UNIT_TILES[u] * P], BF16, tag="h", name="h")
+            e = EXPERT_OF[u]
+            nc.scalar.activation(
+                out=h_tiles[u][:, t, :],
+                in_=first_sums[(u, t)][:],
+                func=GELU,
+                bias=b1_cols[:, e, t : t + 1],
+            )
+
+        def interleave_h(u):
+            h_grouped[u] = work.tile(
+                [P, UNIT_TILES[u] * P * PACK], BF16, tag="hg", name="hg", align_bytes=64
+            )
+            nc.vector.tensor_copy(
+                out=h_grouped[u][:].rearrange("p (n t) -> p n t", t=PACK),
+                in_=h_tiles[u][:].rearrange("p t n -> p n t"),
+            )
 
         def second_product(u, a):
-            second_sums[(u, a)] = multiply(h_mx[u], a, w2_codes, w2_planes, u // UNITS_PER_EXPERT)
-
-        def shared_out(u, a):
-            return u % 2 == 0 and a == 0
-
-        def add_b2_beside_vector(u, a):
-            nc.scalar.copy(out=results[u][:, a, :], in_=second_sums[(u, a)][:])
-            nc.gpsimd.tensor_tensor(
-                out=results[u][:, a, :],
-                in0=results[u][:, a, :],
-                in1=b2_rows[:, u // UNITS_PER_EXPERT, :],
-                op=ADD,
+            e = EXPERT_OF[u]
+            codes, plane = h_mx[u]
+            cols = slice(P * a, P * (a + 1))
+            acc = psum.tile([P, WIDTH], F32, tag="second", name="second", bufs=3)
+            nc.tensor.matmul_mx(
+                out=acc[:],
+                lhsT=codes[:, cols].bitcast(FP8X4),
+                lhsT_scale=plane[:, cols],
+                rhs=w2_codes[:, e, :].bitcast(FP8X4),
+                rhs_scale=w2_planes[PLANE_ROWS * e : P, :],
+                start=True,
+                stop=True,
             )
+            second_sums[(u, a)] = acc
+
+        def handed_over(u, a):
+            return UNIT_TILES[u] == 4 and a == 2
 
         def add_b2(u, a):
-            nc.vector.tensor_tensor(
-                out=results[u][:, a, :],
-                in0=second_sums[(u, a)][:],
-                in1=b2_rows[:, u // UNITS_PER_EXPERT, :],
-                op=ADD,
-            )
+            b2_row = b2_rows[:, EXPERT_OF[u], :]
+            if handed_over(u, a):
+                nc.scalar.copy(out=results[u][:, a, :], in_=second_sums[(u, a)][:])
+                nc.gpsimd.tensor_tensor(
+                    out=results[u][:, a, :], in0=results[u][:, a, :], in1=b2_row, op=ADD
+                )
+            else:
+                nc.vector.tensor_tensor(
+                    out=results[u][:, a, :], in0=second_sums[(u, a)][:], in1=b2_row, op=ADD
+                )
 
         def store(u):
-            nc.sync.dma_start(
-                out=out_units[u],
-                in_=results[u][:].rearrange("p a n -> p (a n)"),
-            )
+            nc.sync.dma_start(out=rows_of(out, u), in_=results[u][:].rearrange("p a n -> p (a n)"))
 
-        for s in range(-4, UNITS + 7):
-            if is_unit(s - 1):
-                gelu(s - 1)
-            if is_unit(s - 6):
-                results[s - 6] = work.tile(
-                    [P, TILES, WIDTH], F32, tag="result", name="result", bufs=4
-                )
-                for a in range(TILES):
-                    if shared_out(s - 6, a):
-                        add_b2_beside_vector(s - 6, a)
-            if is_unit(s + 3):
-                x_grouped[s + 3] = regroup(x_banks[s + 3], "x_grouped")
-            if is_unit(s - 3):
-                h_grouped[s - 3] = regroup(h_banks[s - 3], "h_grouped")
-            for a in range(TILES):
-                if is_unit(s):
-                    add_b1(s, a)
-                if is_unit(s + 1):
-                    first_product(s + 1, a)
-            if is_unit(s + 4):
-                x_banks[s + 4] = transpose_words(x_words(s + 4), "xt")
+        for s in range(-2, UNITS + 2):
             if is_unit(s - 2):
-                h_banks[s - 2] = transpose_words(h_words(s - 2), "ht")
-            if is_unit(s - 4):
-                h_mx[s - 4] = quantise(h_grouped[s - 4], "h")
+                results[s - 2] = work.tile(
+                    [P, UNIT_TILES[s - 2], WIDTH], F32, tag="result", name="result", bufs=4
+                )
+            for j in range(4):
+                if is_unit(s):
+                    first_product(s, j)
+                if is_unit(s - 2) and j < UNIT_TILES[s - 2]:
+                    second_product(s - 2, j)
+                if is_unit(s):
+                    gelu(s, j)
+                if is_unit(s + 1) and j < UNIT_TILES[s + 1] // 2:
+                    regroup_x(s + 1, j)
+                if is_unit(s - 2) and j < UNIT_TILES[s - 2]:
+                    add_b2(s - 2, j)
+                if j == 0 and is_unit(s - 1):
+                    interleave_h(s - 1)
+                if j == 1 and is_unit(s - 1):
+                    h_mx[s - 1] = quantise(h_grouped[s - 1], s - 1, "h")
+                if j == 2 and is_unit(s + 1):
+                    x_mx[s + 1] = quantise(x_grouped[s + 1], s + 1, "x")
+                    if s >= 0 and EXPERT_OF[s + 1] != EXPERT_OF[s]:
+                        sort_codes(EXPERT_OF[s + 1])
             if is_unit(s + 2):
-                x_mx[s + 2] = quantise(x_grouped[s + 2], "x")
-            for a in range(TILES):
-                if is_unit(s - 6) and not shared_out(s - 6, a):
-                    add_b2(s - 6, a)
-                if is_unit(s - 5):
-                    second_product(s - 5, a)
-            if is_unit(s - 6):
-                store(s - 6)
+                transpose_x(s + 2)
+            if is_unit(s - 2):
+                store(s - 2)

@@ -177,14 +177,20 @@ def tile_fusedthorexpert_t_e_kernel(
                 bias=b1_cols[:, e, t : t + 1],
             )
 
-        def interleave_h(u):
-            h_grouped[u] = work.tile(
-                [P, UNIT_TILES[u] * P * PACK], BF16, tag="hg", name="hg", align_bytes=64
-            )
-            nc.vector.tensor_copy(
-                out=h_grouped[u][:].rearrange("p (n t) -> p n t", t=PACK),
-                in_=h_tiles[u][:].rearrange("p t n -> p n t"),
-            )
+        def interleave_h(u, engine):
+            if engine == "vector":
+                h_grouped[u] = work.tile(
+                    [P, UNIT_TILES[u] * P * PACK], BF16, tag="hg", name="hg", align_bytes=64
+                )
+            tokens = UNIT_TILES[u] * P
+            split = 3 * P if UNIT_TILES[u] == 4 else tokens
+            cols = slice(0, split) if engine == "vector" else slice(split, tokens)
+            dst = h_grouped[u][:].rearrange("p (n t) -> p n t", t=PACK)[:, cols, :]
+            src = h_tiles[u][:].rearrange("p t n -> p n t")[:, cols, :]
+            if engine == "vector":
+                nc.vector.tensor_copy(out=dst, in_=src)
+            elif split < tokens:
+                nc.scalar.copy(out=dst, in_=src)
 
         def second_product(u, a):
             e = EXPERT_OF[u]
@@ -202,20 +208,13 @@ def tile_fusedthorexpert_t_e_kernel(
             )
             second_sums[(u, a)] = acc
 
-        def handed_over(u, a):
-            return UNIT_TILES[u] == 4 and a == 2
-
         def add_b2(u, a):
-            b2_row = b2_rows[:, EXPERT_OF[u], :]
-            if handed_over(u, a):
-                nc.scalar.copy(out=results[u][:, a, :], in_=second_sums[(u, a)][:])
-                nc.gpsimd.tensor_tensor(
-                    out=results[u][:, a, :], in0=results[u][:, a, :], in1=b2_row, op=ADD
-                )
-            else:
-                nc.vector.tensor_tensor(
-                    out=results[u][:, a, :], in0=second_sums[(u, a)][:], in1=b2_row, op=ADD
-                )
+            nc.vector.tensor_tensor(
+                out=results[u][:, a, :],
+                in0=second_sums[(u, a)][:],
+                in1=b2_rows[:, EXPERT_OF[u], :],
+                op=ADD,
+            )
 
         def store(u):
             nc.sync.dma_start(out=rows_of(out, u), in_=results[u][:].rearrange("p a n -> p (a n)"))
@@ -232,12 +231,13 @@ def tile_fusedthorexpert_t_e_kernel(
                     second_product(s - 2, j)
                 if is_unit(s):
                     gelu(s, j)
-                if is_unit(s + 1) and j < UNIT_TILES[s + 1] // 2:
-                    regroup_x(s + 1, j)
                 if is_unit(s - 2) and j < UNIT_TILES[s - 2]:
                     add_b2(s - 2, j)
                 if j == 0 and is_unit(s - 1):
-                    interleave_h(s - 1)
+                    interleave_h(s - 1, "vector")
+                    interleave_h(s - 1, "scalar")
+                if is_unit(s + 1) and j < UNIT_TILES[s + 1] // 2:
+                    regroup_x(s + 1, j)
                 if j == 1 and is_unit(s - 1):
                     h_mx[s - 1] = quantise(h_grouped[s - 1], s - 1, "h")
                 if j == 2 and is_unit(s + 1):

@@ -11,6 +11,11 @@ U8 = mybir.dt.uint8
 FP8X4 = mybir.dt.float8_e4m3fn_x4
 GELU = mybir.ActivationFunctionType.Gelu
 ADD = mybir.AluOpType.add
+MULT = mybir.AluOpType.mult
+GPS_SHARE = 0
+HEAD = 3
+TAIL = 99
+SCA_SHARE = 192
 
 P = 128
 PACK = 4
@@ -86,9 +91,9 @@ def tile_fusedthorexpert_t_e_kernel(
         load_planes(w1_planes_raw, w1_scales)
         nc.scalar.dma_start(out=b1_cols[:], in_=b1.rearrange("e (p t) -> p e t", t=PACK))
         load_x(1)
+        load_x(2)
         load_codes(w2_codes, w2_words, 0)
         load_planes(w2_planes, w2_scales)
-        load_x(2)
         nc.sync.dma_start(
             out=b2_rows[:].rearrange("p e i -> p (e i)"),
             in_=b2.rearrange("e i -> (e i)").partition_broadcast(P),
@@ -109,8 +114,6 @@ def tile_fusedthorexpert_t_e_kernel(
             out=w1_planes[:].rearrange("p (t m) -> p t m", t=PACK),
             in_=w1_planes_raw[:].rearrange("p (m t) -> p t m", t=PACK),
         )
-        sort_codes(0)
-
         x_banks, x_grouped, x_mx, first_sums = {}, {}, {}, {}
         h_tiles, h_grouped, h_mx, second_sums, results = {}, {}, {}, {}, {}
 
@@ -120,7 +123,8 @@ def tile_fusedthorexpert_t_e_kernel(
         def transpose_x(u):
             for a in range(UNIT_TILES[u]):
                 if a % 2 == 0:
-                    bank = psum.tile([P, 2, 2, P], F32, tag="xt", name="xt", bufs=2)
+                    shape = [P, min(2, UNIT_TILES[u] - a), 2, P]
+                    bank = psum.tile(shape, F32, tag="xt", name="xt", bufs=2)
                     x_banks[(u, a // 2)] = bank
                 words = x_tiles[u][:, a, :].bitcast(F32)
                 for w in range(2):
@@ -133,10 +137,12 @@ def tile_fusedthorexpert_t_e_kernel(
                 x_grouped[u] = work.tile(
                     [P, UNIT_TILES[u] * P * PACK], BF16, tag="xg", name="xg", align_bytes=64
                 )
-            size = 2 * P * PACK
-            part = x_grouped[u][:, size * half : size * (half + 1)]
-            nc.scalar.copy(
-                out=part.bitcast(F32).rearrange("p (a t w) -> p a t w", a=2, w=2),
+            tiles = min(2, UNIT_TILES[u] - 2 * half)
+            size = P * PACK
+            part = x_grouped[u][:, size * 2 * half : size * (2 * half + tiles)]
+            copy = nc.vector.tensor_copy if u < HEAD else nc.scalar.copy
+            copy(
+                out=part.bitcast(F32).rearrange("p (a t w) -> p a t w", a=tiles, w=2),
                 in_=x_banks[(u, half)][:].rearrange("p a w t -> p a t w"),
             )
 
@@ -178,19 +184,31 @@ def tile_fusedthorexpert_t_e_kernel(
             )
 
         def interleave_h(u, engine):
-            if engine == "vector":
+            if u not in h_grouped:
                 h_grouped[u] = work.tile(
                     [P, UNIT_TILES[u] * P * PACK], BF16, tag="hg", name="hg", align_bytes=64
                 )
             tokens = UNIT_TILES[u] * P
-            split = 3 * P if UNIT_TILES[u] == 4 else tokens
-            cols = slice(0, split) if engine == "vector" else slice(split, tokens)
+            by_gpsimd = GPS_SHARE if UNIT_TILES[u] == 4 else 0
+            by_scalar = SCA_SHARE if UNIT_TILES[u] == 4 else 0
+            by_vector = tokens - by_gpsimd - by_scalar
+            cols = {
+                "gpsimd": slice(0, by_gpsimd),
+                "vector": slice(by_gpsimd, by_gpsimd + by_vector),
+                "scalar": slice(tokens - by_scalar, tokens),
+            }[engine]
+            if cols.start == cols.stop:
+                return
             dst = h_grouped[u][:].rearrange("p (n t) -> p n t", t=PACK)[:, cols, :]
             src = h_tiles[u][:].rearrange("p t n -> p n t")[:, cols, :]
             if engine == "vector":
                 nc.vector.tensor_copy(out=dst, in_=src)
-            elif split < tokens:
+            elif engine == "scalar":
                 nc.scalar.copy(out=dst, in_=src)
+            else:
+                nc.gpsimd.tensor_scalar(
+                    out=dst, in0=src, scalar1=1.0, scalar2=0.0, op0=MULT, op1=ADD
+                )
 
         def second_product(u, a):
             e = EXPERT_OF[u]
@@ -209,6 +227,15 @@ def tile_fusedthorexpert_t_e_kernel(
             second_sums[(u, a)] = acc
 
         def add_b2(u, a):
+            if (u >= TAIL and a % 2 == 1) if UNIT_TILES[u] > 1 else u == UNITS - 2:
+                nc.scalar.copy(out=results[u][:, a, :], in_=second_sums[(u, a)][:])
+                nc.gpsimd.tensor_tensor(
+                    out=results[u][:, a, :],
+                    in0=results[u][:, a, :],
+                    in1=b2_rows[:, EXPERT_OF[u], :],
+                    op=ADD,
+                )
+                return
             nc.vector.tensor_tensor(
                 out=results[u][:, a, :],
                 in0=second_sums[(u, a)][:],
@@ -222,28 +249,31 @@ def tile_fusedthorexpert_t_e_kernel(
         for s in range(-2, UNITS + 2):
             if is_unit(s - 2):
                 results[s - 2] = work.tile(
-                    [P, UNIT_TILES[s - 2], WIDTH], F32, tag="result", name="result", bufs=4
+                    [P, UNIT_TILES[s - 2], WIDTH], F32, tag="result", name="result", bufs=6
                 )
             for j in range(4):
                 if is_unit(s):
                     first_product(s, j)
                 if is_unit(s - 2) and j < UNIT_TILES[s - 2]:
                     second_product(s - 2, j)
+                if j == 0 and is_unit(s + 1):
+                    for half in range((UNIT_TILES[s + 1] + 1) // 2):
+                        regroup_x(s + 1, half)
                 if is_unit(s):
                     gelu(s, j)
+                if j == 0 and is_unit(s - 1):
+                    interleave_h(s - 1, "gpsimd")
+                    interleave_h(s - 1, "scalar")
                 if is_unit(s - 2) and j < UNIT_TILES[s - 2]:
                     add_b2(s - 2, j)
                 if j == 0 and is_unit(s - 1):
                     interleave_h(s - 1, "vector")
-                    interleave_h(s - 1, "scalar")
-                if is_unit(s + 1) and j < UNIT_TILES[s + 1] // 2:
-                    regroup_x(s + 1, j)
+                if j == 0 and is_unit(s + 1):
+                    if s < 0 or EXPERT_OF[s + 1] != EXPERT_OF[s]:
+                        sort_codes(EXPERT_OF[s + 1])
+                    x_mx[s + 1] = quantise(x_grouped[s + 1], s + 1, "x")
                 if j == 1 and is_unit(s - 1):
                     h_mx[s - 1] = quantise(h_grouped[s - 1], s - 1, "h")
-                if j == 2 and is_unit(s + 1):
-                    x_mx[s + 1] = quantise(x_grouped[s + 1], s + 1, "x")
-                    if s >= 0 and EXPERT_OF[s + 1] != EXPERT_OF[s]:
-                        sort_codes(EXPERT_OF[s + 1])
             if is_unit(s + 2):
                 transpose_x(s + 2)
             if is_unit(s - 2):

@@ -12,10 +12,10 @@ FP8X4 = mybir.dt.float8_e4m3fn_x4
 GELU = mybir.ActivationFunctionType.Gelu
 ADD = mybir.AluOpType.add
 MULT = mybir.AluOpType.mult
-GPS_SHARE = 0
+GPS_SHARE = 192
 HEAD = 3
 TAIL = 99
-SCA_SHARE = 192
+SCA_SHARE = 128
 
 P = 128
 PACK = 4

@@ -12,10 +12,10 @@ FP8X4 = mybir.dt.float8_e4m3fn_x4
 GELU = mybir.ActivationFunctionType.Gelu
 ADD = mybir.AluOpType.add
 MULT = mybir.AluOpType.mult
-GPS_SHARE = 192
+GPS_SHARE = 256
 HEAD = 3
 TAIL = 99
-SCA_SHARE = 128
+SCA_SHARE = 96
 
 P = 128
 PACK = 4
@@ -25,7 +25,7 @@ WORDS = WIDTH // 2
 TOKENS = 8192
 PLANE_ROWS = 4
 
-UNIT_TILES = [2, 2, 4, 4, 4] + [4] * 8 + [4, 4, 4, 2, 2]
+UNIT_TILES = [4] * 15 + [2, 2]
 UNITS = len(UNIT_TILES)
 FIRST_TILE = [sum(UNIT_TILES[:u]) for u in range(UNITS)]
 EXPERT_OF = [FIRST_TILE[u] // 16 for u in range(UNITS)]
@@ -189,8 +189,8 @@ def tile_fusedthorexpert_t_e_kernel(
                     [P, UNIT_TILES[u] * P * PACK], BF16, tag="hg", name="hg", align_bytes=64
                 )
             tokens = UNIT_TILES[u] * P
-            by_gpsimd = GPS_SHARE if UNIT_TILES[u] == 4 else 0
-            by_scalar = SCA_SHARE if UNIT_TILES[u] == 4 else 0
+            by_gpsimd = GPS_SHARE if UNIT_TILES[u] == 4 and u < UNITS - 2 else 0
+            by_scalar = (SCA_SHARE if UNIT_TILES[u] == 4 else 0) if u < UNITS-2 else tokens
             by_vector = tokens - by_gpsimd - by_scalar
             cols = {
                 "gpsimd": slice(0, by_gpsimd),

@@ -12,10 +12,10 @@ FP8X4 = mybir.dt.float8_e4m3fn_x4
 GELU = mybir.ActivationFunctionType.Gelu
 ADD = mybir.AluOpType.add
 MULT = mybir.AluOpType.mult
-GPS_SHARE = 256
+GPS_SHARE = 384
 HEAD = 3
 TAIL = 99
-SCA_SHARE = 96
+SCA_SHARE = 64
 
 P = 128
 PACK = 4
@@ -186,7 +186,7 @@ def tile_fusedthorexpert_t_e_kernel(
         def interleave_h(u, engine):
             if u not in h_grouped:
                 h_grouped[u] = work.tile(
-                    [P, UNIT_TILES[u] * P * PACK], BF16, tag="hg", name="hg", align_bytes=64
+                    [P, UNIT_TILES[u] * P * PACK], BF16, tag="hg", name="hg", bufs=1, align_bytes=64
                 )
             tokens = UNIT_TILES[u] * P
             by_gpsimd = GPS_SHARE if UNIT_TILES[u] == 4 and u < UNITS - 2 else 0
@@ -266,9 +266,9 @@ def tile_fusedthorexpert_t_e_kernel(
                     interleave_h(s - 1, "scalar")
                 if is_unit(s - 2) and j < UNIT_TILES[s - 2]:
                     add_b2(s - 2, j)
-                if j == 0 and is_unit(s - 1):
+                if j == 1 and is_unit(s - 1):
                     interleave_h(s - 1, "vector")
-                if j == 0 and is_unit(s + 1):
+                if j == 1 and is_unit(s + 1):
                     if s < 0 or EXPERT_OF[s + 1] != EXPERT_OF[s]:
                         sort_codes(EXPERT_OF[s + 1])
                     x_mx[s + 1] = quantise(x_grouped[s + 1], s + 1, "x")

@@ -199,8 +199,9 @@ def tile_fusedthorexpert_t_e_kernel(
             }[engine]
             if cols.start == cols.stop:
                 return
-            dst = h_grouped[u][:].rearrange("p (n t) -> p n t", t=PACK)[:, cols, :]
-            src = h_tiles[u][:].rearrange("p t n -> p n t")[:, cols, :]
+            words = slice(PACK * cols.start, PACK * cols.stop)
+            dst = h_grouped[u][:, words].rearrange("p (c i t) -> p c t i", i=4, t=PACK)
+            src = h_tiles[u][:, :, cols].rearrange("p t (c i) -> p c t i", i=4)
             if engine == "vector":
                 nc.vector.tensor_copy(out=dst, in_=src)
             elif engine == "scalar":

@@ -44,7 +44,7 @@ def tile_fusedthorexpert_t_e_kernel(
 
     with ExitStack() as ctx:
         keep = ctx.enter_context(tc.tile_pool(name="keep", bufs=1))
-        work = ctx.enter_context(tc.tile_pool(name="work", bufs=2))
+        work = ctx.enter_context(tc.tile_pool(name="work", bufs=3))
         psum = ctx.enter_context(tc.psum_pool(name="psum", bufs=2))
         ctx.enter_context(tc.manual_schedule())
 
@@ -186,7 +186,7 @@ def tile_fusedthorexpert_t_e_kernel(
         def interleave_h(u, engine):
             if u not in h_grouped:
                 h_grouped[u] = work.tile(
-                    [P, UNIT_TILES[u] * P * PACK], BF16, tag="hg", name="hg", bufs=1, align_bytes=64
+                    [P, UNIT_TILES[u] * P * PACK], BF16, tag="hg", name="hg", bufs=2, align_bytes=64
                 )
             tokens = UNIT_TILES[u] * P
             by_gpsimd = GPS_SHARE if UNIT_TILES[u] == 4 and u < UNITS - 2 else 0
@@ -250,7 +250,7 @@ def tile_fusedthorexpert_t_e_kernel(
         for s in range(-2, UNITS + 2):
             if is_unit(s - 2):
                 results[s - 2] = work.tile(
-                    [P, UNIT_TILES[s - 2], WIDTH], F32, tag="result", name="result", bufs=6
+                    [P, UNIT_TILES[s - 2], WIDTH], F32, tag="result", name="result", bufs=8
                 )
             for j in range(4):
                 if is_unit(s):

from contextlib import ExitStack

import concourse.mybir as mybir
from concourse.masks import make_identity

F32 = mybir.dt.float32
BF16 = mybir.dt.bfloat16
I32 = mybir.dt.int32
U32 = mybir.dt.uint32
U8 = mybir.dt.uint8
FP8X4 = mybir.dt.float8_e4m3fn_x4
GELU = mybir.ActivationFunctionType.Gelu
ADD = mybir.AluOpType.add
MULT = mybir.AluOpType.mult
GPS_SHARE = 384
HEAD = 3
TAIL = 99
SCA_SHARE = 64

P = 128
PACK = 4
EXPERTS = 4
WIDTH = 512
WORDS = WIDTH // 2
TOKENS = 8192
PLANE_ROWS = 4

UNIT_TILES = [4] * 15 + [2, 2]
UNITS = len(UNIT_TILES)
FIRST_TILE = [sum(UNIT_TILES[:u]) for u in range(UNITS)]
EXPERT_OF = [FIRST_TILE[u] // 16 for u in range(UNITS)]

FLOPS = 2 * 2 * TOKENS * WIDTH * WIDTH


def tile_fusedthorexpert_t_e_kernel(
    tc, x, w1_words, w1_scales, b1, w2_words, w2_scales, b2, out
):
    nc = tc.nc

    def rows_of(array, u):
        rows = slice(P * FIRST_TILE[u], P * (FIRST_TILE[u] + UNIT_TILES[u]))
        return array[rows, :].rearrange("(p a) k -> p (a k)", p=P)

    with ExitStack() as ctx:
        keep = ctx.enter_context(tc.tile_pool(name="keep", bufs=1))
        work = ctx.enter_context(tc.tile_pool(name="work", bufs=3))
        psum = ctx.enter_context(tc.psum_pool(name="psum", bufs=2))
        ctx.enter_context(tc.manual_schedule())

        ident = keep.tile([P, P], F32)
        make_identity(nc, ident[:])

        w1_planes_raw = keep.tile([P, WIDTH], U8, align_bytes=64)
        w1_planes = keep.tile([P, WIDTH], U8, align_bytes=64)
        w2_planes = keep.tile([P, WIDTH], U8, align_bytes=64)
        nc.vector.memset(w1_planes_raw[:].bitcast(I32), 0)
        nc.vector.memset(w2_planes[:].bitcast(I32), 0)
        w1_raw = keep.tile([P, EXPERTS, WIDTH], I32, align_bytes=64)
        w1_codes = keep.tile([P, EXPERTS, WIDTH], I32, align_bytes=64)
        w2_codes = keep.tile([P, EXPERTS, WIDTH], I32, align_bytes=64)
        b1_cols = keep.tile([P, EXPERTS, PACK], BF16)
        b2_rows = keep.tile([P, EXPERTS, WIDTH], BF16)
        x_tiles = [
            keep.tile([P, UNIT_TILES[u], WIDTH], BF16, name="x%d" % u) for u in range(UNITS)
        ]

        def load_x(u):
            nc.sync.dma_start(out=x_tiles[u][:].rearrange("p a k -> p (a k)"), in_=rows_of(x, u))

        def load_codes(codes, words, e):
            nc.sync.dma_start(
                out=codes[:, e, :], in_=words[e].rearrange("p n t -> p (n t)").bitcast(I32)
            )

        def load_planes(planes, scales):
            for quadrant in range(4):
                rows = slice(PLANE_ROWS * quadrant, PLANE_ROWS * (quadrant + 1))
                first = 32 * quadrant
                nc.sync.dma_start(
                    out=planes[first : first + EXPERTS * PLANE_ROWS, :].bitcast(I32),
                    in_=scales[:, rows, :].bitcast(I32),
                )

        warm = keep.tile([P, 1], F32)
        nc.vector.memset(warm[:], 0.0)
        nc.scalar.activation(out=warm[:], in_=warm[:], func=GELU)

        load_x(0)
        load_codes(w1_raw, w1_words, 0)
        load_planes(w1_planes_raw, w1_scales)
        nc.scalar.dma_start(out=b1_cols[:], in_=b1.rearrange("e (p t) -> p e t", t=PACK))
        load_x(1)
        load_x(2)
        load_codes(w2_codes, w2_words, 0)
        load_planes(w2_planes, w2_scales)
        nc.sync.dma_start(
            out=b2_rows[:].rearrange("p e i -> p (e i)"),
            in_=b2.rearrange("e i -> (e i)").partition_broadcast(P),
        )
        for u in range(3, UNITS):
            if EXPERT_OF[u] != EXPERT_OF[u - 1]:
                load_codes(w1_raw, w1_words, EXPERT_OF[u])
                load_codes(w2_codes, w2_words, EXPERT_OF[u])
            load_x(u)

        def sort_codes(e):
            nc.vector.tensor_copy(
                out=w1_codes[:, e, :].rearrange("p (t m) -> p t m", t=PACK),
                in_=w1_raw[:, e, :].rearrange("p (m t) -> p t m", t=PACK),
            )

        nc.vector.tensor_copy(
            out=w1_planes[:].rearrange("p (t m) -> p t m", t=PACK),
            in_=w1_planes_raw[:].rearrange("p (m t) -> p t m", t=PACK),
        )
        x_banks, x_grouped, x_mx, first_sums = {}, {}, {}, {}
        h_tiles, h_grouped, h_mx, second_sums, results = {}, {}, {}, {}, {}

        def is_unit(u):
            return 0 <= u < UNITS

        def transpose_x(u):
            for a in range(UNIT_TILES[u]):
                if a % 2 == 0:
                    shape = [P, min(2, UNIT_TILES[u] - a), 2, P]
                    bank = psum.tile(shape, F32, tag="xt", name="xt", bufs=2)
                    x_banks[(u, a // 2)] = bank
                words = x_tiles[u][:, a, :].bitcast(F32)
                for w in range(2):
                    nc.tensor.transpose(
                        out=bank[:, a % 2, w, :], in_=words[:, w:WORDS:2], identity=ident[:]
                    )

        def regroup_x(u, half):
            if half == 0:
                x_grouped[u] = work.tile(
                    [P, UNIT_TILES[u] * P * PACK], BF16, tag="xg", name="xg", align_bytes=64
                )
            tiles = min(2, UNIT_TILES[u] - 2 * half)
            size = P * PACK
            part = x_grouped[u][:, size * 2 * half : size * (2 * half + tiles)]
            copy = nc.vector.tensor_copy if u < HEAD else nc.scalar.copy
            copy(
                out=part.bitcast(F32).rearrange("p (a t w) -> p a t w", a=tiles, w=2),
                in_=x_banks[(u, half)][:].rearrange("p a w t -> p a t w"),
            )

        def quantise(grouped, u, tag):
            codes = work.tile(
                [P, UNIT_TILES[u] * P], U32, tag=tag + "_codes", name=tag + "_codes", align_bytes=64
            )
            plane = work.tile(
                [P, UNIT_TILES[u] * P], U8, tag=tag + "_plane", name=tag + "_plane", align_bytes=64
            )
            nc.vector.quantize_mx(out=codes[:].bitcast(FP8X4), scales=plane[:], in_=grouped[:])
            return codes, plane

        def first_product(u, t):
            e = EXPERT_OF[u]
            codes, plane = x_mx[u]
            cols = slice(P * t, P * (t + 1))
            acc = psum.tile([P, UNIT_TILES[u] * P], F32, tag="first", name="first", bufs=3)
            nc.tensor.matmul_mx(
                out=acc[:],
                lhsT=w1_codes[:, e, cols].bitcast(FP8X4),
                lhsT_scale=w1_planes[PLANE_ROWS * e : P, cols],
                rhs=codes[:].bitcast(FP8X4),
                rhs_scale=plane[:],
                start=True,
                stop=True,
            )
            first_sums[(u, t)] = acc

        def gelu(u, t):
            if t == 0:
                h_tiles[u] = work.tile([P, PACK, UNIT_TILES[u] * P], BF16, tag="h", name="h")
            e = EXPERT_OF[u]
            nc.scalar.activation(
                out=h_tiles[u][:, t, :],
                in_=first_sums[(u, t)][:],
                func=GELU,
                bias=b1_cols[:, e, t : t + 1],
            )

        def interleave_h(u, engine):
            if u not in h_grouped:
                h_grouped[u] = work.tile(
                    [P, UNIT_TILES[u] * P * PACK], BF16, tag="hg", name="hg", bufs=2, align_bytes=64
                )
            tokens = UNIT_TILES[u] * P
            by_gpsimd = GPS_SHARE if UNIT_TILES[u] == 4 and u < UNITS - 2 else 0
            by_scalar = (SCA_SHARE if UNIT_TILES[u] == 4 else 0) if u < UNITS-2 else tokens
            by_vector = tokens - by_gpsimd - by_scalar
            cols = {
                "gpsimd": slice(0, by_gpsimd),
                "vector": slice(by_gpsimd, by_gpsimd + by_vector),
                "scalar": slice(tokens - by_scalar, tokens),
            }[engine]
            if cols.start == cols.stop:
                return
            words = slice(PACK * cols.start, PACK * cols.stop)
            dst = h_grouped[u][:, words].rearrange("p (c i t) -> p c t i", i=4, t=PACK)
            src = h_tiles[u][:, :, cols].rearrange("p t (c i) -> p c t i", i=4)
            if engine == "vector":
                nc.vector.tensor_copy(out=dst, in_=src)
            elif engine == "scalar":
                nc.scalar.copy(out=dst, in_=src)
            else:
                nc.gpsimd.tensor_scalar(
                    out=dst, in0=src, scalar1=1.0, scalar2=0.0, op0=MULT, op1=ADD
                )

        def second_product(u, a):
            e = EXPERT_OF[u]
            codes, plane = h_mx[u]
            cols = slice(P * a, P * (a + 1))
            acc = psum.tile([P, WIDTH], F32, tag="second", name="second", bufs=3)
            nc.tensor.matmul_mx(
                out=acc[:],
                lhsT=codes[:, cols].bitcast(FP8X4),
                lhsT_scale=plane[:, cols],
                rhs=w2_codes[:, e, :].bitcast(FP8X4),
                rhs_scale=w2_planes[PLANE_ROWS * e : P, :],
                start=True,
                stop=True,
            )
            second_sums[(u, a)] = acc

        def add_b2(u, a):
            if (u >= TAIL and a % 2 == 1) if UNIT_TILES[u] > 1 else u == UNITS - 2:
                nc.scalar.copy(out=results[u][:, a, :], in_=second_sums[(u, a)][:])
                nc.gpsimd.tensor_tensor(
                    out=results[u][:, a, :],
                    in0=results[u][:, a, :],
                    in1=b2_rows[:, EXPERT_OF[u], :],
                    op=ADD,
                )
                return
            nc.vector.tensor_tensor(
                out=results[u][:, a, :],
                in0=second_sums[(u, a)][:],
                in1=b2_rows[:, EXPERT_OF[u], :],
                op=ADD,
            )

        def store(u):
            nc.sync.dma_start(out=rows_of(out, u), in_=results[u][:].rearrange("p a n -> p (a n)"))

        for s in range(-2, UNITS + 2):
            if is_unit(s - 2):
                results[s - 2] = work.tile(
                    [P, UNIT_TILES[s - 2], WIDTH], F32, tag="result", name="result", bufs=8
                )
            for j in range(4):
                if is_unit(s):
                    first_product(s, j)
                if is_unit(s - 2) and j < UNIT_TILES[s - 2]:
                    second_product(s - 2, j)
                if j == 0 and is_unit(s + 1):
                    for half in range((UNIT_TILES[s + 1] + 1) // 2):
                        regroup_x(s + 1, half)
                if is_unit(s):
                    gelu(s, j)
                if j == 0 and is_unit(s - 1):
                    interleave_h(s - 1, "gpsimd")
                    interleave_h(s - 1, "scalar")
                if is_unit(s - 2) and j < UNIT_TILES[s - 2]:
                    add_b2(s - 2, j)
                if j == 1 and is_unit(s - 1):
                    interleave_h(s - 1, "vector")
                if j == 1 and is_unit(s + 1):
                    if s < 0 or EXPERT_OF[s + 1] != EXPERT_OF[s]:
                        sort_codes(EXPERT_OF[s + 1])
                    x_mx[s + 1] = quantise(x_grouped[s + 1], s + 1, "x")
                if j == 1 and is_unit(s - 1):
                    h_mx[s - 1] = quantise(h_grouped[s - 1], s - 1, "h")
            if is_unit(s + 2):
                transpose_x(s + 2)
            if is_unit(s - 2):
                store(s - 2)
